import numpy as np
import ml_dtypes


def mxq(x, axis, fmt="e4m3"):
    dtype, down = {"e4m3": (ml_dtypes.float8_e4m3fn, 7), "e5m2": (ml_dtypes.float8_e5m2, 14)}[fmt]
    v = np.moveaxis(np.asarray(x, np.float32).astype(ml_dtypes.bfloat16).astype(np.float64), axis, -1)
    blocks = v.reshape(v.shape[:-1] + (-1, 32))
    amax = np.abs(blocks).max(-1, keepdims=True)
    byte = np.maximum(np.where(amax > 0, np.frexp(amax)[1] - 1 + 127, 0) - down, 1)
    scale = np.exp2(byte - 127.0)
    codes = (blocks / scale).astype(np.float32).astype(dtype).astype(np.float64)
    return np.moveaxis((codes * scale).reshape(v.shape), -1, axis)


WIDE = False


def mx_kscale(k):
    if not WIDE:
        return np.ones(k)
    levels = np.array([20, -20, 10, -10, 0])
    a = np.random.permutation(np.resize(levels, k // 512 * 4)).reshape(k // 512, 4)
    idx = np.arange(k)
    return np.exp2(a[idx // 512, idx % 128 // 32])


BF16 = ml_dtypes.bfloat16


def bf(x):
    return np.asarray(x, np.float32).astype(BF16)


def f64(x):
    return np.asarray(x).astype(np.float64)


B, N_IN, N_OUT, D_IN, D_OUT = 1024, 4, 32, 1024, 16
K = N_OUT * D_OUT


def setup_inputs():
    s = mx_kscale(K).reshape(N_OUT, D_OUT)
    inputs = np.random.standard_normal((B, N_IN, D_IN, 1))
    transform_mat = np.random.uniform(-1.0, 1.0, (1, N_IN, N_OUT, D_IN, D_OUT, 1)) * np.sqrt(3.0 / D_IN) / s[None, None, :, None, :, None]
    g = np.random.standard_normal((B, N_IN, N_OUT, D_OUT, 1)) * np.exp2(np.random.randint(-12, 1, (B, N_IN, 1, 1, 1))) * 8.0 * s[None, None, :, :, None]
    return {"inputs": bf(inputs), "transform_mat": bf(transform_mat), "grad_out": bf(g)}


def reference(inputs, transform_mat, grad_out):
    g = f64(grad_out)[..., 0].reshape(B, N_IN, K)
    w = f64(transform_mat)[0, ..., 0].transpose(0, 2, 1, 3).reshape(N_IN, D_IN, K)
    gq = mxq(g, 2, "e5m2")
    wq = mxq(w, 2, "e4m3")
    prod = gq.transpose(1, 0, 2) @ wq.transpose(0, 2, 1)
    return prod.transpose(1, 0, 2)[..., None]

@@ -1,0 +1,176 @@
+from contextlib import ExitStack
+
+import concourse.bass as bass
+import concourse.mybir as mybir
+import concourse.tile as tile
+from concourse.masks import make_identity
+
+F32 = mybir.dt.float32
+BF16 = mybir.dt.bfloat16
+U32 = mybir.dt.uint32
+U8 = mybir.dt.uint8
+E4X4 = mybir.dt.float8_e4m3fn_x4
+E5X4 = mybir.dt.float8_e5m2_x4
+
+P = 128
+B = 1024
+N_IN = 4
+D_IN = 1024
+K = 512
+BT = B // P
+
+FLOPS = 2 * B * N_IN * D_IN * K
+BYTES = 2 * B * N_IN * K + 2 * N_IN * D_IN * K + 4 * B * N_IN * D_IN
+
+PINNED = False
+
+
+def tile_transforming_t_kernel(tc, inputs, transform_mat, grad_out, out):
+    nc = tc.nc
+    w_dram = transform_mat.rearrange("a n m (h l) o x -> (a n) (m h) (l o x)", h=4)
+    g_dram = grad_out.rearrange("(t p) n m o x -> t p (n m o x)", p=P)
+    o_dram = out.rearrange("(t p) n i x -> t p (n i x)", p=P)
+
+    with ExitStack() as ctx:
+        keep = ctx.enter_context(tc.tile_pool(name="keep", bufs=1))
+        work = ctx.enter_context(tc.tile_pool(name="work", bufs=2))
+        stage = ctx.enter_context(tc.tile_pool(name="stage", bufs=8))
+        tps = ctx.enter_context(tc.psum_pool(name="tps", bufs=4))
+        acc = ctx.enter_context(tc.psum_pool(name="acc", bufs=4))
+        if PINNED:
+            ctx.enter_context(tc.manual_schedule())
+
+        ident = keep.tile([P, P], F32, name="ident")
+        make_identity(nc, ident[:])
+
+        w_raw = [keep.tile([P, 4096], BF16, name="w_raw%d" % n) for n in range(N_IN)]
+        g_raw = [keep.tile([P, 2048], BF16, name="g_raw%d" % t) for t in range(BT)]
+        w_codes = [keep.tile([P, D_IN], U32, name="w_codes%d" % n, align_bytes=64) for n in range(N_IN)]
+        w_scales = [keep.tile([P, D_IN], U8, name="w_scales%d" % n, align_bytes=64) for n in range(N_IN)]
+        g_codes = [keep.tile([P, N_IN * P], U32, name="g_codes%d" % t, align_bytes=64) for t in range(BT)]
+        g_scales = [keep.tile([P, N_IN * P], U8, name="g_scales%d" % t, align_bytes=64) for t in range(BT)]
+
+        def load_w(n):
+            nc.sync.dma_start(out=w_raw[n][:], in_=w_dram[n])
+
+        def load_g(t):
+            nc.sync.dma_start(out=g_raw[t][:], in_=g_dram[t])
+
+        load_w(0)
+        load_w(1)
+        for t in range(BT):
+            load_g(t)
+        load_w(2)
+        load_w(3)
+
+        busy = {"v": 0, "s": 0}
+
+        def copy_on(eng, dst, src):
+            busy[eng] += 512
+            if eng == "v":
+                nc.vector.tensor_copy(out=dst, in_=src)
+            else:
+                nc.scalar.copy(out=dst, in_=src)
+
+        def idle_engine():
+            return "v" if busy["v"] < busy["s"] else "s"
+
+        mid = {}
+
+        def w_stage1(n):
+            words = w_raw[n][:].bitcast(F32).rearrange("p (h j o) -> p h j o", h=2, o=8)
+            s2 = work.tile([P, 2048], F32, name="s2")
+            mid[n] = s2
+            s2v = s2[:].rearrange("p (a h m o) -> p a h m o", a=4, h=2, o=8)
+            for h in range(2):
+                eng = idle_engine()
+                for og in range(2):
+                    bank = tps.tile([P, 4, P], F32, name="tp")
+                    for oo in range(4):
+                        nc.tensor.transpose(bank[:, oo, :], words[:, h, :, og * 4 + oo], ident[:])
+                    copy_on(
+                        eng,
+                        s2v[:, :, h, :, og * 4 : og * 4 + 4],
+                        bank[:].rearrange("p o (m a) -> p a m o", a=4),
+                    )
+
+        def w_stage2(n):
+            s2v = mid[n][:].rearrange("p (a h u q) -> p a h u q", a=4, h=2, u=2)
+            grouped = work.tile([P, 4096], BF16, name="w_grouped", align_bytes=64)
+            gv = grouped[:].bitcast(F32).rearrange("p (a h j u) -> p a h j u", a=4, h=2, u=2)
+            for a in range(4):
+                bank = tps.tile([P, 2, 2, P], F32, name="tp")
+                for h in range(2):
+                    for u in range(2):
+                        nc.tensor.transpose(bank[:, h, u, :], s2v[:, a, h, u, :], ident[:])
+                copy_on(idle_engine(), gv[:, a], bank[:].rearrange("p h u j -> p h j u"))
+            for half in range(2):
+                busy["v"] += 560
+                nc.vector.quantize_mx(
+                    out=w_codes[n][:, half * 512 : half * 512 + 512].bitcast(E4X4),
+                    scales=w_scales[n][:, half * 512 : half * 512 + 512],
+                    in_=grouped[:, half * 2048 : half * 2048 + 2048],
+                )
+
+        def g_prep(t):
+            words = g_raw[t][:].bitcast(F32).rearrange("p (n u q) -> p n u q", n=N_IN, u=2)
+            grouped = work.tile([P, 2048], BF16, name="g_grouped", align_bytes=64)
+            gv = grouped[:].bitcast(F32).rearrange("p (c n b u) -> p c n b u", c=2, n=2, u=2)
+            for c in range(2):
+                bank = tps.tile([P, 2, 2, P], F32, name="tp")
+                for n in range(2):
+                    for u in range(2):
+                        nc.tensor.transpose(bank[:, n, u, :], words[:, 2 * c + n, u, :], ident[:])
+                copy_on(idle_engine(), gv[:, c], bank[:].rearrange("p n u b -> p n b u"))
+            busy["v"] += 560
+            nc.vector.quantize_mx(
+                out=g_codes[t][:].bitcast(E5X4),
+                scales=g_scales[t][:],
+                in_=grouped[:],
+            )
+
+        def mm(t, pair):
+            res = stage.tile([P, 2048], F32, name="res")
+            for n2 in range(2):
+                n = 2 * pair + n2
+                for half in range(2):
+                    ps = acc.tile([P, 512], F32, name="ps")
+                    nc.tensor.matmul_mx(
+                        out=ps[:],
+                        lhsT=g_codes[t][:, n * P : n * P + P].bitcast(E5X4),
+                        lhsT_scale=g_scales[t][:, n * P : n * P + P],
+                        rhs=w_codes[n][:, half * 512 : half * 512 + 512].bitcast(E4X4),
+                        rhs_scale=w_scales[n][:, half * 512 : half * 512 + 512],
+                        start=True,
+                        stop=True,
+                    )
+                    col = n2 * 1024 + half * 512
+                    copy_on(idle_engine(), res[:, col : col + 512], ps[:])
+            nc.sync.dma_start(out=o_dram[t][:, pair * 2048 : pair * 2048 + 2048], in_=res[:])
+
+        w_stage1(0)
+        w_stage1(1)
+        w_stage2(0)
+        w_stage2(1)
+        g_prep(0)
+        g_prep(1)
+        mm(0, 0)
+        mm(1, 0)
+        g_prep(2)
+        g_prep(3)
+        mm(2, 0)
+        mm(3, 0)
+        w_stage1(2)
+        w_stage1(3)
+        g_prep(4)
+        g_prep(5)
+        mm(4, 0)
+        mm(5, 0)
+        w_stage2(2)
+        w_stage2(3)
+        g_prep(6)
+        g_prep(7)
+        mm(6, 0)
+        mm(7, 0)
+        for t in range(BT):
+            mm(t, 1)

@@ -1,8 +1,6 @@
 from contextlib import ExitStack
 
-import concourse.bass as bass
 import concourse.mybir as mybir
-import concourse.tile as tile
 from concourse.masks import make_identity
 
 F32 = mybir.dt.float32
@@ -22,19 +20,20 @@ BT = B // P
 FLOPS = 2 * B * N_IN * D_IN * K
 BYTES = 2 * B * N_IN * K + 2 * N_IN * D_IN * K + 4 * B * N_IN * D_IN
 
-PINNED = False
+PINNED = True
 
 
 def tile_transforming_t_kernel(tc, inputs, transform_mat, grad_out, out):
     nc = tc.nc
     w_dram = transform_mat.rearrange("a n m (h l) o x -> (a n) (m h) (l o x)", h=4)
     g_dram = grad_out.rearrange("(t p) n m o x -> t p (n m o x)", p=P)
-    o_dram = out.rearrange("(t p) n i x -> t p (n i x)", p=P)
+    o_dram = out.rearrange("(t p) n i x -> t p n (i x)", p=P)
 
     with ExitStack() as ctx:
         keep = ctx.enter_context(tc.tile_pool(name="keep", bufs=1))
         work = ctx.enter_context(tc.tile_pool(name="work", bufs=2))
-        stage = ctx.enter_context(tc.tile_pool(name="stage", bufs=8))
+        gwork = ctx.enter_context(tc.tile_pool(name="gwork", bufs=4))
+        stage = ctx.enter_context(tc.tile_pool(name="stage", bufs=16))
         tps = ctx.enter_context(tc.psum_pool(name="tps", bufs=4))
         acc = ctx.enter_context(tc.psum_pool(name="acc", bufs=4))
         if PINNED:
@@ -50,30 +49,18 @@ def tile_transforming_t_kernel(tc, inputs, transform_mat, grad_out, out):
         g_codes = [keep.tile([P, N_IN * P], U32, name="g_codes%d" % t, align_bytes=64) for t in range(BT)]
         g_scales = [keep.tile([P, N_IN * P], U8, name="g_scales%d" % t, align_bytes=64) for t in range(BT)]
 
-        def load_w(n):
+        for h in range(2):
+            nc.sync.dma_start(out=w_raw[0][:, h * 2048 : h * 2048 + 2048], in_=w_dram[0][:, h * 2048 : h * 2048 + 2048])
+        for t in range(BT):
+            nc.sync.dma_start(out=g_raw[t][:], in_=g_dram[t])
+        for n in range(1, N_IN):
             nc.sync.dma_start(out=w_raw[n][:], in_=w_dram[n])
 
-        def load_g(t):
-            nc.sync.dma_start(out=g_raw[t][:], in_=g_dram[t])
-
-        load_w(0)
-        load_w(1)
-        for t in range(BT):
-            load_g(t)
-        load_w(2)
-        load_w(3)
-
-        busy = {"v": 0, "s": 0}
-
-        def copy_on(eng, dst, src):
-            busy[eng] += 512
-            if eng == "v":
-                nc.vector.tensor_copy(out=dst, in_=src)
-            else:
+        def empty_bank(index, dst, src):
+            if index % 2 == 0:
                 nc.scalar.copy(out=dst, in_=src)
-
-        def idle_engine():
-            return "v" if busy["v"] < busy["s"] else "s"
+            else:
+                nc.vector.tensor_copy(out=dst, in_=src)
 
         mid = {}
 
@@ -83,13 +70,12 @@ def tile_transforming_t_kernel(tc, inputs, transform_mat, grad_out, out):
             mid[n] = s2
             s2v = s2[:].rearrange("p (a h m o) -> p a h m o", a=4, h=2, o=8)
             for h in range(2):
-                eng = idle_engine()
                 for og in range(2):
                     bank = tps.tile([P, 4, P], F32, name="tp")
                     for oo in range(4):
                         nc.tensor.transpose(bank[:, oo, :], words[:, h, :, og * 4 + oo], ident[:])
-                    copy_on(
-                        eng,
+                    empty_bank(
+                        0,
                         s2v[:, :, h, :, og * 4 : og * 4 + 4],
                         bank[:].rearrange("p o (m a) -> p a m o", a=4),
                     )
@@ -103,74 +89,59 @@ def tile_transforming_t_kernel(tc, inputs, transform_mat, grad_out, out):
                 for h in range(2):
                     for u in range(2):
                         nc.tensor.transpose(bank[:, h, u, :], s2v[:, a, h, u, :], ident[:])
-                copy_on(idle_engine(), gv[:, a], bank[:].rearrange("p h u j -> p h j u"))
+                empty_bank(a, gv[:, a], bank[:].rearrange("p h u j -> p h j u"))
             for half in range(2):
-                busy["v"] += 560
                 nc.vector.quantize_mx(
                     out=w_codes[n][:, half * 512 : half * 512 + 512].bitcast(E4X4),
                     scales=w_scales[n][:, half * 512 : half * 512 + 512],
                     in_=grouped[:, half * 2048 : half * 2048 + 2048],
                 )
 
-        def g_prep(t):
-            words = g_raw[t][:].bitcast(F32).rearrange("p (n u q) -> p n u q", n=N_IN, u=2)
-            grouped = work.tile([P, 2048], BF16, name="g_grouped", align_bytes=64)
-            gv = grouped[:].bitcast(F32).rearrange("p (c n b u) -> p c n b u", c=2, n=2, u=2)
-            for c in range(2):
-                bank = tps.tile([P, 2, 2, P], F32, name="tp")
-                for n in range(2):
-                    for u in range(2):
-                        nc.tensor.transpose(bank[:, n, u, :], words[:, 2 * c + n, u, :], ident[:])
-                copy_on(idle_engine(), gv[:, c], bank[:].rearrange("p n u b -> p n b u"))
-            busy["v"] += 560
-            nc.vector.quantize_mx(
-                out=g_codes[t][:].bitcast(E5X4),
-                scales=g_scales[t][:],
-                in_=grouped[:],
-            )
+        def g_prep_two(t0):
+            grouped = {}
+            for t in (t0, t0 + 1):
+                words = g_raw[t][:].bitcast(F32).rearrange("p (n u q) -> p n u q", n=N_IN, u=2)
+                grouped[t] = gwork.tile([P, 2048], BF16, name="g_grouped", align_bytes=64)
+                gv = grouped[t][:].bitcast(F32).rearrange("p (c n b u) -> p c n b u", c=2, n=2, u=2)
+                for c in range(2):
+                    bank = tps.tile([P, 2, 2, P], F32, name="tp")
+                    for n in range(2):
+                        for u in range(2):
+                            nc.tensor.transpose(bank[:, n, u, :], words[:, 2 * c + n, u, :], ident[:])
+                    empty_bank(c, gv[:, c], bank[:].rearrange("p n u b -> p n b u"))
+            for t in (t0, t0 + 1):
+                nc.vector.quantize_mx(
+                    out=g_codes[t][:].bitcast(E5X4),
+                    scales=g_scales[t][:],
+                    in_=grouped[t][:],
+                )
 
-        def mm(t, pair):
-            res = stage.tile([P, 2048], F32, name="res")
-            for n2 in range(2):
-                n = 2 * pair + n2
-                for half in range(2):
-                    ps = acc.tile([P, 512], F32, name="ps")
-                    nc.tensor.matmul_mx(
-                        out=ps[:],
-                        lhsT=g_codes[t][:, n * P : n * P + P].bitcast(E5X4),
-                        lhsT_scale=g_scales[t][:, n * P : n * P + P],
-                        rhs=w_codes[n][:, half * 512 : half * 512 + 512].bitcast(E4X4),
-                        rhs_scale=w_scales[n][:, half * 512 : half * 512 + 512],
-                        start=True,
-                        stop=True,
-                    )
-                    col = n2 * 1024 + half * 512
-                    copy_on(idle_engine(), res[:, col : col + 512], ps[:])
-            nc.sync.dma_start(out=o_dram[t][:, pair * 2048 : pair * 2048 + 2048], in_=res[:])
+        def mm(t, n):
+            res = stage.tile([P, D_IN], F32, name="res")
+            for half in range(2):
+                ps = acc.tile([P, 512], F32, name="ps")
+                nc.tensor.matmul_mx(
+                    out=ps[:],
+                    lhsT=g_codes[t][:, n * P : n * P + P].bitcast(E5X4),
+                    lhsT_scale=g_scales[t][:, n * P : n * P + P],
+                    rhs=w_codes[n][:, half * 512 : half * 512 + 512].bitcast(E4X4),
+                    rhs_scale=w_scales[n][:, half * 512 : half * 512 + 512],
+                    start=True,
+                    stop=True,
+                )
+                empty_bank(half, res[:, half * 512 : half * 512 + 512], ps[:])
+            nc.sync.dma_start(out=o_dram[t][:, n, :], in_=res[:])
 
         w_stage1(0)
-        w_stage1(1)
+        g_prep_two(0)
         w_stage2(0)
-        w_stage2(1)
-        g_prep(0)
-        g_prep(1)
-        mm(0, 0)
-        mm(1, 0)
-        g_prep(2)
-        g_prep(3)
-        mm(2, 0)
-        mm(3, 0)
-        w_stage1(2)
-        w_stage1(3)
-        g_prep(4)
-        g_prep(5)
-        mm(4, 0)
-        mm(5, 0)
-        w_stage2(2)
-        w_stage2(3)
-        g_prep(6)
-        g_prep(7)
-        mm(6, 0)
-        mm(7, 0)
-        for t in range(BT):
-            mm(t, 1)
+        g_prep_two(2)
+        for n in range(N_IN):
+            for t in range(BT):
+                mm(t, n)
+                if n == 0 and t in (1, 3):
+                    g_prep_two(t + 3)
+                if n + 1 < N_IN and t == 4:
+                    w_stage1(n + 1)
+                if n + 1 < N_IN and t == 6:
+                    w_stage2(n + 1)

@@ -20,7 +20,7 @@ BT = B // P
 FLOPS = 2 * B * N_IN * D_IN * K
 BYTES = 2 * B * N_IN * K + 2 * N_IN * D_IN * K + 4 * B * N_IN * D_IN
 
-PINNED = True
+WARM = False
 
 
 def tile_transforming_t_kernel(tc, inputs, transform_mat, grad_out, out):
@@ -31,14 +31,15 @@ def tile_transforming_t_kernel(tc, inputs, transform_mat, grad_out, out):
 
     with ExitStack() as ctx:
         keep = ctx.enter_context(tc.tile_pool(name="keep", bufs=1))
-        work = ctx.enter_context(tc.tile_pool(name="work", bufs=2))
-        gwork = ctx.enter_context(tc.tile_pool(name="gwork", bufs=4))
+        work = ctx.enter_context(tc.tile_pool(name="work", bufs=4))
         stage = ctx.enter_context(tc.tile_pool(name="stage", bufs=16))
         tps = ctx.enter_context(tc.psum_pool(name="tps", bufs=4))
         acc = ctx.enter_context(tc.psum_pool(name="acc", bufs=4))
-        if PINNED:
-            ctx.enter_context(tc.manual_schedule())
+        ctx.enter_context(tc.manual_schedule())
 
+        if WARM:
+            zeros = keep.tile([P, 512], BF16, name="zeros")
+            nc.vector.memset(zeros[:], 0.0)
         ident = keep.tile([P, P], F32, name="ident")
         make_identity(nc, ident[:])
 
@@ -62,46 +63,53 @@ def tile_transforming_t_kernel(tc, inputs, transform_mat, grad_out, out):
             else:
                 nc.vector.tensor_copy(out=dst, in_=src)
 
+        def warm(count):
+            if WARM:
+                for unused in range(count):
+                    ps = acc.tile([P, 512], F32, name="ps")
+                    nc.tensor.matmul(ps[:], lhsT=zeros[:, 0:P], rhs=zeros[:], start=True, stop=True)
+
         mid = {}
 
-        def w_stage1(n):
+        def w_stage1(n, h):
             words = w_raw[n][:].bitcast(F32).rearrange("p (h j o) -> p h j o", h=2, o=8)
-            s2 = work.tile([P, 2048], F32, name="s2")
-            mid[n] = s2
-            s2v = s2[:].rearrange("p (a h m o) -> p a h m o", a=4, h=2, o=8)
-            for h in range(2):
-                for og in range(2):
-                    bank = tps.tile([P, 4, P], F32, name="tp")
-                    for oo in range(4):
-                        nc.tensor.transpose(bank[:, oo, :], words[:, h, :, og * 4 + oo], ident[:])
-                    empty_bank(
-                        0,
-                        s2v[:, :, h, :, og * 4 : og * 4 + 4],
-                        bank[:].rearrange("p o (m a) -> p a m o", a=4),
-                    )
-
-        def w_stage2(n):
-            s2v = mid[n][:].rearrange("p (a h u q) -> p a h u q", a=4, h=2, u=2)
-            grouped = work.tile([P, 4096], BF16, name="w_grouped", align_bytes=64)
-            gv = grouped[:].bitcast(F32).rearrange("p (a h j u) -> p a h j u", a=4, h=2, u=2)
-            for a in range(4):
-                bank = tps.tile([P, 2, 2, P], F32, name="tp")
-                for h in range(2):
-                    for u in range(2):
-                        nc.tensor.transpose(bank[:, h, u, :], s2v[:, a, h, u, :], ident[:])
-                empty_bank(a, gv[:, a], bank[:].rearrange("p h u j -> p h j u"))
-            for half in range(2):
-                nc.vector.quantize_mx(
-                    out=w_codes[n][:, half * 512 : half * 512 + 512].bitcast(E4X4),
-                    scales=w_scales[n][:, half * 512 : half * 512 + 512],
-                    in_=grouped[:, half * 2048 : half * 2048 + 2048],
+            s2 = work.tile([P, 1024], F32, name="s2")
+            mid[(n, h)] = s2
+            s2v = s2[:].rearrange("p (a m o) -> p a m o", a=4, o=8)
+            for og in range(2):
+                bank = tps.tile([P, 4, P], F32, name="tp")
+                for oo in range(4):
+                    nc.tensor.transpose(bank[:, oo, :], words[:, h, :, og * 4 + oo], ident[:])
+                empty_bank(
+                    0,
+                    s2v[:, :, :, og * 4 : og * 4 + 4],
+                    bank[:].rearrange("p o (m a) -> p a m o", a=4),
                 )
+
+        def w_stage2(n, h):
+            s2v = mid[(n, h)][:].rearrange("p (a u q) -> p a u q", a=4, u=2)
+            grouped = work.tile([P, 2048], BF16, name="w_grouped", align_bytes=64)
+            gv = grouped[:].bitcast(F32).rearrange("p (c a j u) -> p c a j u", c=2, a=2, u=2)
+            for c in range(2):
+                bank = tps.tile([P, 2, 2, P], F32, name="tp")
+                for a in range(2):
+                    for u in range(2):
+                        nc.tensor.transpose(bank[:, a, u, :], s2v[:, 2 * c + a, u, :], ident[:])
+                empty_bank(c, gv[:, c], bank[:].rearrange("p a u j -> p a j u"))
+            return grouped
+
+        def w_quantise(n, h, grouped):
+            nc.vector.quantize_mx(
+                out=w_codes[n][:, h * 512 : h * 512 + 512].bitcast(E4X4),
+                scales=w_scales[n][:, h * 512 : h * 512 + 512],
+                in_=grouped[:],
+            )
 
         def g_prep_two(t0):
             grouped = {}
             for t in (t0, t0 + 1):
                 words = g_raw[t][:].bitcast(F32).rearrange("p (n u q) -> p n u q", n=N_IN, u=2)
-                grouped[t] = gwork.tile([P, 2048], BF16, name="g_grouped", align_bytes=64)
+                grouped[t] = work.tile([P, 2048], BF16, name="g_grouped", align_bytes=64)
                 gv = grouped[t][:].bitcast(F32).rearrange("p (c n b u) -> p c n b u", c=2, n=2, u=2)
                 for c in range(2):
                     bank = tps.tile([P, 2, 2, P], F32, name="tp")
@@ -118,30 +126,44 @@ def tile_transforming_t_kernel(tc, inputs, transform_mat, grad_out, out):
 
         def mm(t, n):
             res = stage.tile([P, D_IN], F32, name="res")
-            for half in range(2):
+            resv = res[:].rearrange("p (a h j) -> p a h j", a=4, h=2)
+            for h in range(2):
                 ps = acc.tile([P, 512], F32, name="ps")
                 nc.tensor.matmul_mx(
                     out=ps[:],
                     lhsT=g_codes[t][:, n * P : n * P + P].bitcast(E5X4),
                     lhsT_scale=g_scales[t][:, n * P : n * P + P],
-                    rhs=w_codes[n][:, half * 512 : half * 512 + 512].bitcast(E4X4),
-                    rhs_scale=w_scales[n][:, half * 512 : half * 512 + 512],
+                    rhs=w_codes[n][:, h * 512 : h * 512 + 512].bitcast(E4X4),
+                    rhs_scale=w_scales[n][:, h * 512 : h * 512 + 512],
                     start=True,
                     stop=True,
                 )
-                empty_bank(half, res[:, half * 512 : half * 512 + 512], ps[:])
+                empty_bank(h, resv[:, :, h, :], ps[:].rearrange("p (a j) -> p a j", a=4))
             nc.sync.dma_start(out=o_dram[t][:, n, :], in_=res[:])
 
-        w_stage1(0)
+        warm(7)
+        w_stage1(0, 0)
+        warm(1)
+        w_stage1(0, 1)
+        warm(1)
         g_prep_two(0)
-        w_stage2(0)
+        warm(1)
+        first0 = w_stage2(0, 0)
+        first1 = w_stage2(0, 1)
+        w_quantise(0, 0, first0)
+        w_quantise(0, 1, first1)
+        warm(1)
         g_prep_two(2)
         for n in range(N_IN):
             for t in range(BT):
                 mm(t, n)
                 if n == 0 and t in (1, 3):
                     g_prep_two(t + 3)
-                if n + 1 < N_IN and t == 4:
-                    w_stage1(n + 1)
-                if n + 1 < N_IN and t == 6:
-                    w_stage2(n + 1)
+                if n + 1 < N_IN:
+                    if t == 4:
+                        w_stage1(n + 1, 0)
+                    if t == 5:
+                        w_stage1(n + 1, 1)
+                        w_quantise(n + 1, 0, w_stage2(n + 1, 0))
+                    if t == 6:
+                        w_quantise(n + 1, 1, w_stage2(n + 1, 1))

@@ -20,7 +20,7 @@ BT = B // P
 FLOPS = 2 * B * N_IN * D_IN * K
 BYTES = 2 * B * N_IN * K + 2 * N_IN * D_IN * K + 4 * B * N_IN * D_IN
 
-WARM = False
+PINNED = True
 
 
 def tile_transforming_t_kernel(tc, inputs, transform_mat, grad_out, out):
@@ -31,15 +31,14 @@ def tile_transforming_t_kernel(tc, inputs, transform_mat, grad_out, out):
 
     with ExitStack() as ctx:
         keep = ctx.enter_context(tc.tile_pool(name="keep", bufs=1))
-        work = ctx.enter_context(tc.tile_pool(name="work", bufs=4))
+        work = ctx.enter_context(tc.tile_pool(name="work", bufs=2))
+        gwork = ctx.enter_context(tc.tile_pool(name="gwork", bufs=4))
         stage = ctx.enter_context(tc.tile_pool(name="stage", bufs=16))
         tps = ctx.enter_context(tc.psum_pool(name="tps", bufs=4))
         acc = ctx.enter_context(tc.psum_pool(name="acc", bufs=4))
-        ctx.enter_context(tc.manual_schedule())
+        if PINNED:
+            ctx.enter_context(tc.manual_schedule())
 
-        if WARM:
-            zeros = keep.tile([P, 512], BF16, name="zeros")
-            nc.vector.memset(zeros[:], 0.0)
         ident = keep.tile([P, P], F32, name="ident")
         make_identity(nc, ident[:])
 
@@ -63,60 +62,53 @@ def tile_transforming_t_kernel(tc, inputs, transform_mat, grad_out, out):
             else:
                 nc.vector.tensor_copy(out=dst, in_=src)
 
-        def warm(count):
-            if WARM:
-                for unused in range(count):
-                    ps = acc.tile([P, 512], F32, name="ps")
-                    nc.tensor.matmul(ps[:], lhsT=zeros[:, 0:P], rhs=zeros[:], start=True, stop=True)
-
         mid = {}
 
-        def w_stage1(n, h):
+        def w_stage1(n):
             words = w_raw[n][:].bitcast(F32).rearrange("p (h j o) -> p h j o", h=2, o=8)
-            s2 = work.tile([P, 1024], F32, name="s2")
-            mid[(n, h)] = s2
-            s2v = s2[:].rearrange("p (a m o) -> p a m o", a=4, o=8)
-            for og in range(2):
-                bank = tps.tile([P, 4, P], F32, name="tp")
-                for oo in range(4):
-                    nc.tensor.transpose(bank[:, oo, :], words[:, h, :, og * 4 + oo], ident[:])
-                empty_bank(
-                    0,
-                    s2v[:, :, :, og * 4 : og * 4 + 4],
-                    bank[:].rearrange("p o (m a) -> p a m o", a=4),
-                )
+            s2 = work.tile([P, 2048], F32, name="s2")
+            mid[n] = s2
+            s2v = s2[:].rearrange("p (a h m o) -> p a h m o", a=4, h=2, o=8)
+            for h in range(2):
+                for og in range(2):
+                    bank = tps.tile([P, 4, P], F32, name="tp")
+                    for oo in range(4):
+                        nc.tensor.transpose(bank[:, oo, :], words[:, h, :, og * 4 + oo], ident[:])
+                    empty_bank(
+                        h,
+                        s2v[:, :, h, :, og * 4 : og * 4 + 4],
+                        bank[:].rearrange("p o (m a) -> p a m o", a=4),
+                    )
 
-        def w_stage2(n, h):
-            s2v = mid[(n, h)][:].rearrange("p (a u q) -> p a u q", a=4, u=2)
-            grouped = work.tile([P, 2048], BF16, name="w_grouped", align_bytes=64)
-            gv = grouped[:].bitcast(F32).rearrange("p (c a j u) -> p c a j u", c=2, a=2, u=2)
-            for c in range(2):
+        def w_stage2(n):
+            s2v = mid[n][:].rearrange("p (a h u q) -> p a h u q", a=4, h=2, u=2)
+            grouped = work.tile([P, 4096], BF16, name="w_grouped", align_bytes=64)
+            gv = grouped[:].bitcast(F32).rearrange("p (a h j u) -> p a h j u", a=4, h=2, u=2)
+            for a in range(4):
                 bank = tps.tile([P, 2, 2, P], F32, name="tp")
-                for a in range(2):
+                for h in range(2):
                     for u in range(2):
-                        nc.tensor.transpose(bank[:, a, u, :], s2v[:, 2 * c + a, u, :], ident[:])
-                empty_bank(c, gv[:, c], bank[:].rearrange("p a u j -> p a j u"))
-            return grouped
-
-        def w_quantise(n, h, grouped):
-            nc.vector.quantize_mx(
-                out=w_codes[n][:, h * 512 : h * 512 + 512].bitcast(E4X4),
-                scales=w_scales[n][:, h * 512 : h * 512 + 512],
-                in_=grouped[:],
-            )
+                        nc.tensor.transpose(bank[:, h, u, :], s2v[:, a, h, u, :], ident[:])
+                empty_bank(a, gv[:, a], bank[:].rearrange("p h u j -> p h j u"))
+            for half in range(2):
+                nc.vector.quantize_mx(
+                    out=w_codes[n][:, half * 512 : half * 512 + 512].bitcast(E4X4),
+                    scales=w_scales[n][:, half * 512 : half * 512 + 512],
+                    in_=grouped[:, half * 2048 : half * 2048 + 2048],
+                )
 
         def g_prep_two(t0):
             grouped = {}
             for t in (t0, t0 + 1):
                 words = g_raw[t][:].bitcast(F32).rearrange("p (n u q) -> p n u q", n=N_IN, u=2)
-                grouped[t] = work.tile([P, 2048], BF16, name="g_grouped", align_bytes=64)
+                grouped[t] = gwork.tile([P, 2048], BF16, name="g_grouped", align_bytes=64)
                 gv = grouped[t][:].bitcast(F32).rearrange("p (c n b u) -> p c n b u", c=2, n=2, u=2)
                 for c in range(2):
                     bank = tps.tile([P, 2, 2, P], F32, name="tp")
                     for n in range(2):
                         for u in range(2):
                             nc.tensor.transpose(bank[:, n, u, :], words[:, 2 * c + n, u, :], ident[:])
-                    empty_bank(c, gv[:, c], bank[:].rearrange("p n u b -> p n b u"))
+                    empty_bank(0, gv[:, c], bank[:].rearrange("p n u b -> p n b u"))
             for t in (t0, t0 + 1):
                 nc.vector.quantize_mx(
                     out=g_codes[t][:].bitcast(E5X4),
@@ -126,44 +118,30 @@ def tile_transforming_t_kernel(tc, inputs, transform_mat, grad_out, out):
 
         def mm(t, n):
             res = stage.tile([P, D_IN], F32, name="res")
-            resv = res[:].rearrange("p (a h j) -> p a h j", a=4, h=2)
-            for h in range(2):
+            for half in range(2):
                 ps = acc.tile([P, 512], F32, name="ps")
                 nc.tensor.matmul_mx(
                     out=ps[:],
                     lhsT=g_codes[t][:, n * P : n * P + P].bitcast(E5X4),
                     lhsT_scale=g_scales[t][:, n * P : n * P + P],
-                    rhs=w_codes[n][:, h * 512 : h * 512 + 512].bitcast(E4X4),
-                    rhs_scale=w_scales[n][:, h * 512 : h * 512 + 512],
+                    rhs=w_codes[n][:, half * 512 : half * 512 + 512].bitcast(E4X4),
+                    rhs_scale=w_scales[n][:, half * 512 : half * 512 + 512],
                     start=True,
                     stop=True,
                 )
-                empty_bank(h, resv[:, :, h, :], ps[:].rearrange("p (a j) -> p a j", a=4))
+                empty_bank(half, res[:, half * 512 : half * 512 + 512], ps[:])
             nc.sync.dma_start(out=o_dram[t][:, n, :], in_=res[:])
 
-        warm(7)
-        w_stage1(0, 0)
-        warm(1)
-        w_stage1(0, 1)
-        warm(1)
+        w_stage1(0)
         g_prep_two(0)
-        warm(1)
-        first0 = w_stage2(0, 0)
-        first1 = w_stage2(0, 1)
-        w_quantise(0, 0, first0)
-        w_quantise(0, 1, first1)
-        warm(1)
+        w_stage2(0)
         g_prep_two(2)
         for n in range(N_IN):
             for t in range(BT):
                 mm(t, n)
                 if n == 0 and t in (1, 3):
                     g_prep_two(t + 3)
-                if n + 1 < N_IN:
-                    if t == 4:
-                        w_stage1(n + 1, 0)
-                    if t == 5:
-                        w_stage1(n + 1, 1)
-                        w_quantise(n + 1, 0, w_stage2(n + 1, 0))
-                    if t == 6:
-                        w_quantise(n + 1, 1, w_stage2(n + 1, 1))
+                if n + 1 < N_IN and t == 4:
+                    w_stage1(n + 1)
+                if n + 1 < N_IN and t == 6:
+                    w_stage2(n + 1)

@@ -39,6 +39,8 @@ def tile_transforming_t_kernel(tc, inputs, transform_mat, grad_out, out):
         if PINNED:
             ctx.enter_context(tc.manual_schedule())
 
+        zeros = keep.tile([P, 512], BF16, name="zeros")
+        nc.vector.memset(zeros[:], 0.0)
         ident = keep.tile([P, P], F32, name="ident")
         make_identity(nc, ident[:])
 
@@ -62,6 +64,11 @@ def tile_transforming_t_kernel(tc, inputs, transform_mat, grad_out, out):
             else:
                 nc.vector.tensor_copy(out=dst, in_=src)
 
+        def warm(count):
+            for unused in range(count):
+                ps = acc.tile([P, 512], F32, name="ps")
+                nc.tensor.matmul(ps[:], lhsT=zeros[:, 0:P], rhs=zeros[:], start=True, stop=True)
+
         mid = {}
 
         def w_stage1(n):
@@ -70,12 +77,14 @@ def tile_transforming_t_kernel(tc, inputs, transform_mat, grad_out, out):
             mid[n] = s2
             s2v = s2[:].rearrange("p (a h m o) -> p a h m o", a=4, h=2, o=8)
             for h in range(2):
+                if n == 0 and h == 1:
+                    warm(1)
                 for og in range(2):
                     bank = tps.tile([P, 4, P], F32, name="tp")
                     for oo in range(4):
                         nc.tensor.transpose(bank[:, oo, :], words[:, h, :, og * 4 + oo], ident[:])
                     empty_bank(
-                        h,
+                        0,
                         s2v[:, :, h, :, og * 4 : og * 4 + 4],
                         bank[:].rearrange("p o (m a) -> p a m o", a=4),
                     )
@@ -108,7 +117,7 @@ def tile_transforming_t_kernel(tc, inputs, transform_mat, grad_out, out):
                     for n in range(2):
                         for u in range(2):
                             nc.tensor.transpose(bank[:, n, u, :], words[:, 2 * c + n, u, :], ident[:])
-                    empty_bank(0, gv[:, c], bank[:].rearrange("p n u b -> p n b u"))
+                    empty_bank(c, gv[:, c], bank[:].rearrange("p n u b -> p n b u"))
             for t in (t0, t0 + 1):
                 nc.vector.quantize_mx(
                     out=g_codes[t][:].bitcast(E5X4),
@@ -132,9 +141,13 @@ def tile_transforming_t_kernel(tc, inputs, transform_mat, grad_out, out):
                 empty_bank(half, res[:, half * 512 : half * 512 + 512], ps[:])
             nc.sync.dma_start(out=o_dram[t][:, n, :], in_=res[:])
 
+        warm(6)
         w_stage1(0)
+        warm(1)
         g_prep_two(0)
+        warm(1)
         w_stage2(0)
+        warm(1)
         g_prep_two(2)
         for n in range(N_IN):
             for t in range(BT):

@@ -16,28 +16,25 @@ N_IN = 4
 D_IN = 1024
 K = 512
 BT = B // P
+BC = BT // 2
 
 FLOPS = 2 * B * N_IN * D_IN * K
 BYTES = 2 * B * N_IN * K + 2 * N_IN * D_IN * K + 4 * B * N_IN * D_IN
-
-PINNED = True
 
 
 def tile_transforming_t_kernel(tc, inputs, transform_mat, grad_out, out):
     nc = tc.nc
     w_dram = transform_mat.rearrange("a n m (h l) o x -> (a n) (m h) (l o x)", h=4)
-    g_dram = grad_out.rearrange("(t p) n m o x -> t p (n m o x)", p=P)
-    o_dram = out.rearrange("(t p) n i x -> t p n (i x)", p=P)
+    g_dram = grad_out.rearrange("(p c t) n m o x -> c p (t n m o x)", c=BC, t=2)
+    o_dram = out.rearrange("(p t) n i x -> t p (n i x)", t=BT)
 
     with ExitStack() as ctx:
         keep = ctx.enter_context(tc.tile_pool(name="keep", bufs=1))
         work = ctx.enter_context(tc.tile_pool(name="work", bufs=2))
-        gwork = ctx.enter_context(tc.tile_pool(name="gwork", bufs=4))
-        stage = ctx.enter_context(tc.tile_pool(name="stage", bufs=16))
-        tps = ctx.enter_context(tc.psum_pool(name="tps", bufs=4))
-        acc = ctx.enter_context(tc.psum_pool(name="acc", bufs=4))
-        if PINNED:
-            ctx.enter_context(tc.manual_schedule())
+        gwork = ctx.enter_context(tc.tile_pool(name="gwork", bufs=3))
+        stage = ctx.enter_context(tc.tile_pool(name="stage", bufs=8))
+        psum = ctx.enter_context(tc.psum_pool(name="psum", bufs=8))
+        ctx.enter_context(tc.manual_schedule())
 
         zeros = keep.tile([P, 512], BF16, name="zeros")
         nc.vector.memset(zeros[:], 0.0)
@@ -45,18 +42,21 @@ def tile_transforming_t_kernel(tc, inputs, transform_mat, grad_out, out):
         make_identity(nc, ident[:])
 
         w_raw = [keep.tile([P, 4096], BF16, name="w_raw%d" % n) for n in range(N_IN)]
-        g_raw = [keep.tile([P, 2048], BF16, name="g_raw%d" % t) for t in range(BT)]
+        g_raw = [keep.tile([P, 4096], BF16, name="g_raw%d" % c) for c in range(BC)]
         w_codes = [keep.tile([P, D_IN], U32, name="w_codes%d" % n, align_bytes=64) for n in range(N_IN)]
         w_scales = [keep.tile([P, D_IN], U8, name="w_scales%d" % n, align_bytes=64) for n in range(N_IN)]
-        g_codes = [keep.tile([P, N_IN * P], U32, name="g_codes%d" % t, align_bytes=64) for t in range(BT)]
-        g_scales = [keep.tile([P, N_IN * P], U8, name="g_scales%d" % t, align_bytes=64) for t in range(BT)]
+        g_codes = [keep.tile([P, 2, 512], U32, name="g_codes%d" % c, align_bytes=64) for c in range(BC)]
+        g_scales = [keep.tile([P, 2, 512], U8, name="g_scales%d" % c, align_bytes=64) for c in range(BC)]
 
         for h in range(2):
             nc.sync.dma_start(out=w_raw[0][:, h * 2048 : h * 2048 + 2048], in_=w_dram[0][:, h * 2048 : h * 2048 + 2048])
-        for t in range(BT):
-            nc.sync.dma_start(out=g_raw[t][:], in_=g_dram[t])
-        for n in range(1, N_IN):
-            nc.sync.dma_start(out=w_raw[n][:], in_=w_dram[n])
+        nc.sync.dma_start(out=w_raw[1][:], in_=w_dram[1])
+        nc.sync.dma_start(out=g_raw[0][:], in_=g_dram[0])
+        nc.sync.dma_start(out=g_raw[1][:], in_=g_dram[1])
+        nc.sync.dma_start(out=w_raw[2][:], in_=w_dram[2])
+        nc.sync.dma_start(out=g_raw[2][:], in_=g_dram[2])
+        nc.sync.dma_start(out=g_raw[3][:], in_=g_dram[3])
+        nc.sync.dma_start(out=w_raw[3][:], in_=w_dram[3])
 
         def empty_bank(index, dst, src):
             if index % 2 == 0:
@@ -66,7 +66,7 @@ def tile_transforming_t_kernel(tc, inputs, transform_mat, grad_out, out):
 
         def warm(count):
             for unused in range(count):
-                ps = acc.tile([P, 512], F32, name="ps")
+                ps = psum.tile([P, 512], F32, name="bank")
                 nc.tensor.matmul(ps[:], lhsT=zeros[:, 0:P], rhs=zeros[:], start=True, stop=True)
 
         mid = {}
@@ -77,14 +77,12 @@ def tile_transforming_t_kernel(tc, inputs, transform_mat, grad_out, out):
             mid[n] = s2
             s2v = s2[:].rearrange("p (a h m o) -> p a h m o", a=4, h=2, o=8)
             for h in range(2):
-                if n == 0 and h == 1:
-                    warm(1)
                 for og in range(2):
-                    bank = tps.tile([P, 4, P], F32, name="tp")
+                    bank = psum.tile([P, 4, P], F32, name="bank")
                     for oo in range(4):
                         nc.tensor.transpose(bank[:, oo, :], words[:, h, :, og * 4 + oo], ident[:])
                     empty_bank(
-                        0,
+                        og,
                         s2v[:, :, h, :, og * 4 : og * 4 + 4],
                         bank[:].rearrange("p o (m a) -> p a m o", a=4),
                     )
@@ -94,7 +92,7 @@ def tile_transforming_t_kernel(tc, inputs, transform_mat, grad_out, out):
             grouped = work.tile([P, 4096], BF16, name="w_grouped", align_bytes=64)
             gv = grouped[:].bitcast(F32).rearrange("p (a h j u) -> p a h j u", a=4, h=2, u=2)
             for a in range(4):
-                bank = tps.tile([P, 2, 2, P], F32, name="tp")
+                bank = psum.tile([P, 2, 2, P], F32, name="bank")
                 for h in range(2):
                     for u in range(2):
                         nc.tensor.transpose(bank[:, h, u, :], s2v[:, a, h, u, :], ident[:])
@@ -106,55 +104,65 @@ def tile_transforming_t_kernel(tc, inputs, transform_mat, grad_out, out):
                     in_=grouped[:, half * 2048 : half * 2048 + 2048],
                 )
 
-        def g_prep_two(t0):
-            grouped = {}
-            for t in (t0, t0 + 1):
-                words = g_raw[t][:].bitcast(F32).rearrange("p (n u q) -> p n u q", n=N_IN, u=2)
-                grouped[t] = gwork.tile([P, 2048], BF16, name="g_grouped", align_bytes=64)
-                gv = grouped[t][:].bitcast(F32).rearrange("p (c n b u) -> p c n b u", c=2, n=2, u=2)
-                for c in range(2):
-                    bank = tps.tile([P, 2, 2, P], F32, name="tp")
-                    for n in range(2):
-                        for u in range(2):
-                            nc.tensor.transpose(bank[:, n, u, :], words[:, 2 * c + n, u, :], ident[:])
-                    empty_bank(c, gv[:, c], bank[:].rearrange("p n u b -> p n b u"))
-            for t in (t0, t0 + 1):
-                nc.vector.quantize_mx(
-                    out=g_codes[t][:].bitcast(E5X4),
-                    scales=g_scales[t][:],
-                    in_=grouped[t][:],
-                )
+        def g_prep(c, pr):
+            words = g_raw[c][:].bitcast(F32).rearrange("p (t n u q) -> p t n u q", t=2, n=N_IN, u=2)
+            grouped = gwork.tile([P, 2048], BF16, name="g_grouped", align_bytes=64)
+            gv = grouped[:].bitcast(F32).rearrange("p (t n b u) -> p t n b u", t=2, n=2, u=2)
+            for tl in range(2):
+                bank = psum.tile([P, 2, 2, P], F32, name="bank")
+                for nl in range(2):
+                    for u in range(2):
+                        nc.tensor.transpose(bank[:, nl, u, :], words[:, tl, 2 * pr + nl, u, :], ident[:])
+                empty_bank(0, gv[:, tl], bank[:].rearrange("p n u b -> p n b u"))
+            nc.vector.quantize_mx(
+                out=g_codes[c][:, pr, :].bitcast(E5X4),
+                scales=g_scales[c][:, pr, :],
+                in_=grouped[:],
+            )
 
-        def mm(t, n):
-            res = stage.tile([P, D_IN], F32, name="res")
-            for half in range(2):
-                ps = acc.tile([P, 512], F32, name="ps")
-                nc.tensor.matmul_mx(
-                    out=ps[:],
-                    lhsT=g_codes[t][:, n * P : n * P + P].bitcast(E5X4),
-                    lhsT_scale=g_scales[t][:, n * P : n * P + P],
-                    rhs=w_codes[n][:, half * 512 : half * 512 + 512].bitcast(E4X4),
-                    rhs_scale=w_scales[n][:, half * 512 : half * 512 + 512],
-                    start=True,
-                    stop=True,
-                )
-                empty_bank(half, res[:, half * 512 : half * 512 + 512], ps[:])
-            nc.sync.dma_start(out=o_dram[t][:, n, :], in_=res[:])
+        def mm(c, pr):
+            for tl in range(2):
+                res = stage.tile([P, 2048], F32, name="res")
+                for nl in range(2):
+                    n = 2 * pr + nl
+                    col = (tl * 2 + nl) * P
+                    for half in range(2):
+                        ps = psum.tile([P, 512], F32, name="bank")
+                        nc.tensor.matmul_mx(
+                            out=ps[:],
+                            lhsT=g_codes[c][:, pr, col : col + P].bitcast(E5X4),
+                            lhsT_scale=g_scales[c][:, pr, col : col + P],
+                            rhs=w_codes[n][:, half * 512 : half * 512 + 512].bitcast(E4X4),
+                            rhs_scale=w_scales[n][:, half * 512 : half * 512 + 512],
+                            start=True,
+                            stop=True,
+                        )
+                        empty_bank(half, res[:, (nl * 2 + half) * 512 : (nl * 2 + half) * 512 + 512], ps[:])
+                nc.sync.dma_start(out=o_dram[2 * c + tl][:, pr * 2048 : pr * 2048 + 2048], in_=res[:])
 
         warm(6)
         w_stage1(0)
         warm(1)
-        g_prep_two(0)
-        warm(1)
         w_stage2(0)
-        warm(1)
-        g_prep_two(2)
-        for n in range(N_IN):
-            for t in range(BT):
-                mm(t, n)
-                if n == 0 and t in (1, 3):
-                    g_prep_two(t + 3)
-                if n + 1 < N_IN and t == 4:
-                    w_stage1(n + 1)
-                if n + 1 < N_IN and t == 6:
-                    w_stage2(n + 1)
+        w_stage1(1)
+        g_prep(0, 0)
+        w_stage2(1)
+        g_prep(1, 0)
+        mm(0, 0)
+        mm(1, 0)
+        w_stage1(2)
+        g_prep(2, 0)
+        w_stage2(2)
+        g_prep(3, 0)
+        mm(2, 0)
+        mm(3, 0)
+        w_stage1(3)
+        g_prep(0, 1)
+        w_stage2(3)
+        g_prep(1, 1)
+        mm(0, 1)
+        mm(1, 1)
+        g_prep(2, 1)
+        g_prep(3, 1)
+        mm(2, 1)
+        mm(3, 1)

@@ -27,6 +27,7 @@ def tile_transforming_t_kernel(tc, inputs, transform_mat, grad_out, out):
     w_dram = transform_mat.rearrange("a n m (h l) o x -> (a n) (m h) (l o x)", h=4)
     g_dram = grad_out.rearrange("(p c t) n m o x -> c p (t n m o x)", c=BC, t=2)
     o_dram = out.rearrange("(p t) n i x -> t p (n i x)", t=BT)
+    o_couple = out.rearrange("(p c t) n i x -> c p t (n i x)", c=BC, t=2)
 
     with ExitStack() as ctx:
         keep = ctx.enter_context(tc.tile_pool(name="keep", bufs=1))
@@ -45,17 +46,17 @@ def tile_transforming_t_kernel(tc, inputs, transform_mat, grad_out, out):
         g_raw = [keep.tile([P, 4096], BF16, name="g_raw%d" % c) for c in range(BC)]
         w_codes = [keep.tile([P, D_IN], U32, name="w_codes%d" % n, align_bytes=64) for n in range(N_IN)]
         w_scales = [keep.tile([P, D_IN], U8, name="w_scales%d" % n, align_bytes=64) for n in range(N_IN)]
-        g_codes = [keep.tile([P, 2, 512], U32, name="g_codes%d" % c, align_bytes=64) for c in range(BC)]
-        g_scales = [keep.tile([P, 2, 512], U8, name="g_scales%d" % c, align_bytes=64) for c in range(BC)]
+        g_codes = [keep.tile([P, 512], U32, name="g_codes%d" % j, align_bytes=64) for j in range(8)]
+        g_scales = [keep.tile([P, 512], U8, name="g_scales%d" % j, align_bytes=64) for j in range(8)]
 
         for h in range(2):
             nc.sync.dma_start(out=w_raw[0][:, h * 2048 : h * 2048 + 2048], in_=w_dram[0][:, h * 2048 : h * 2048 + 2048])
         nc.sync.dma_start(out=w_raw[1][:], in_=w_dram[1])
         nc.sync.dma_start(out=g_raw[0][:], in_=g_dram[0])
         nc.sync.dma_start(out=g_raw[1][:], in_=g_dram[1])
-        nc.sync.dma_start(out=w_raw[2][:], in_=w_dram[2])
         nc.sync.dma_start(out=g_raw[2][:], in_=g_dram[2])
         nc.sync.dma_start(out=g_raw[3][:], in_=g_dram[3])
+        nc.sync.dma_start(out=w_raw[2][:], in_=w_dram[2])
         nc.sync.dma_start(out=w_raw[3][:], in_=w_dram[3])
 
         def empty_bank(index, dst, src):
@@ -104,65 +105,98 @@ def tile_transforming_t_kernel(tc, inputs, transform_mat, grad_out, out):
                     in_=grouped[:, half * 2048 : half * 2048 + 2048],
                 )
 
-        def g_prep(c, pr):
-            words = g_raw[c][:].bitcast(F32).rearrange("p (t n u q) -> p t n u q", t=2, n=N_IN, u=2)
+        def g_words(c):
+            return g_raw[c][:].bitcast(F32).rearrange("p (t n u q) -> p t n u q", t=2, n=N_IN, u=2)
+
+        def g_quantize(slot, grouped):
+            nc.vector.quantize_mx(
+                out=g_codes[slot][:].bitcast(E5X4),
+                scales=g_scales[slot][:],
+                in_=grouped[:],
+            )
+
+        def g_prep_pair(c):
             grouped = gwork.tile([P, 2048], BF16, name="g_grouped", align_bytes=64)
             gv = grouped[:].bitcast(F32).rearrange("p (t n b u) -> p t n b u", t=2, n=2, u=2)
             for tl in range(2):
                 bank = psum.tile([P, 2, 2, P], F32, name="bank")
                 for nl in range(2):
                     for u in range(2):
-                        nc.tensor.transpose(bank[:, nl, u, :], words[:, tl, 2 * pr + nl, u, :], ident[:])
+                        nc.tensor.transpose(bank[:, nl, u, :], g_words(c)[:, tl, nl, u, :], ident[:])
                 empty_bank(0, gv[:, tl], bank[:].rearrange("p n u b -> p n b u"))
-            nc.vector.quantize_mx(
-                out=g_codes[c][:, pr, :].bitcast(E5X4),
-                scales=g_scales[c][:, pr, :],
-                in_=grouped[:],
-            )
+            g_quantize(c, grouped)
 
-        def mm(c, pr):
+        def g_prep_single(cc, n):
+            grouped = gwork.tile([P, 2048], BF16, name="g_grouped", align_bytes=64)
+            gv = grouped[:].bitcast(F32).rearrange("p (c t b u) -> p c t b u", c=2, t=2, u=2)
+            for cl in range(2):
+                bank = psum.tile([P, 2, 2, P], F32, name="bank")
+                for tl in range(2):
+                    for u in range(2):
+                        nc.tensor.transpose(bank[:, tl, u, :], g_words(2 * cc + cl)[:, tl, n, u, :], ident[:])
+                empty_bank(0, gv[:, cl], bank[:].rearrange("p t u b -> p t b u"))
+            g_quantize(2 * n + cc, grouped)
+
+        def product(slot, col, n, half, dst):
+            ps = psum.tile([P, 512], F32, name="bank")
+            nc.tensor.matmul_mx(
+                out=ps[:],
+                lhsT=g_codes[slot][:, col : col + P].bitcast(E5X4),
+                lhsT_scale=g_scales[slot][:, col : col + P],
+                rhs=w_codes[n][:, half * 512 : half * 512 + 512].bitcast(E4X4),
+                rhs_scale=w_scales[n][:, half * 512 : half * 512 + 512],
+                start=True,
+                stop=True,
+            )
+            empty_bank(half, dst, ps[:])
+
+        def mm_pair(c):
             for tl in range(2):
                 res = stage.tile([P, 2048], F32, name="res")
                 for nl in range(2):
-                    n = 2 * pr + nl
-                    col = (tl * 2 + nl) * P
                     for half in range(2):
-                        ps = psum.tile([P, 512], F32, name="bank")
-                        nc.tensor.matmul_mx(
-                            out=ps[:],
-                            lhsT=g_codes[c][:, pr, col : col + P].bitcast(E5X4),
-                            lhsT_scale=g_scales[c][:, pr, col : col + P],
-                            rhs=w_codes[n][:, half * 512 : half * 512 + 512].bitcast(E4X4),
-                            rhs_scale=w_scales[n][:, half * 512 : half * 512 + 512],
-                            start=True,
-                            stop=True,
-                        )
-                        empty_bank(half, res[:, (nl * 2 + half) * 512 : (nl * 2 + half) * 512 + 512], ps[:])
-                nc.sync.dma_start(out=o_dram[2 * c + tl][:, pr * 2048 : pr * 2048 + 2048], in_=res[:])
+                        at = (nl * 2 + half) * 512
+                        product(c, (tl * 2 + nl) * P, nl, half, res[:, at : at + 512])
+                nc.sync.dma_start(out=o_dram[2 * c + tl][:, 0:2048], in_=res[:])
+
+        def mm_single(c, n):
+            res = stage.tile([P, 2048], F32, name="res")
+            for tl in range(2):
+                for half in range(2):
+                    at = (tl * 2 + half) * 512
+                    product(2 * n + c // 2, ((c % 2) * 2 + tl) * P, n, half, res[:, at : at + 512])
+            nc.sync.dma_start(
+                out=o_couple[c][:, :, n * D_IN : n * D_IN + D_IN],
+                in_=res[:].rearrange("p (t i) -> p t i", t=2),
+            )
 
         warm(6)
         w_stage1(0)
         warm(1)
         w_stage2(0)
         w_stage1(1)
-        g_prep(0, 0)
+        g_prep_pair(0)
         w_stage2(1)
-        g_prep(1, 0)
-        mm(0, 0)
-        mm(1, 0)
+        g_prep_pair(1)
+        mm_pair(0)
+        g_prep_pair(2)
+        mm_pair(1)
+        g_prep_pair(3)
         w_stage1(2)
-        g_prep(2, 0)
+        mm_pair(2)
         w_stage2(2)
-        g_prep(3, 0)
-        mm(2, 0)
-        mm(3, 0)
+        g_prep_single(0, 2)
+        mm_pair(3)
+        mm_single(0, 2)
+        g_prep_single(1, 2)
         w_stage1(3)
-        g_prep(0, 1)
+        mm_single(1, 2)
+        mm_single(2, 2)
         w_stage2(3)
-        g_prep(1, 1)
-        mm(0, 1)
-        mm(1, 1)
-        g_prep(2, 1)
-        g_prep(3, 1)
-        mm(2, 1)
-        mm(3, 1)
+        g_prep_single(0, 3)
+        mm_single(3, 2)
+        mm_single(0, 3)
+        g_prep_single(1, 3)
+        mm_single(1, 3)
+        mm_single(2, 3)
+        mm_single(3, 3)

@@ -42,8 +42,8 @@ def tile_transforming_t_kernel(tc, inputs, transform_mat, grad_out, out):
         ident = keep.tile([P, P], F32, name="ident")
         make_identity(nc, ident[:])
 
-        w_raw = [keep.tile([P, 4096], BF16, name="w_raw%d" % n) for n in range(N_IN)]
-        g_raw = [keep.tile([P, 4096], BF16, name="g_raw%d" % c) for c in range(BC)]
+        w_raw = [keep.tile([P, 4096], BF16, name="w_raw%d" % n, align_bytes=256) for n in range(N_IN)]
+        g_raw = [keep.tile([P, 4096], BF16, name="g_raw%d" % c, align_bytes=256) for c in range(BC)]
         w_codes = [keep.tile([P, D_IN], U32, name="w_codes%d" % n, align_bytes=64) for n in range(N_IN)]
         w_scales = [keep.tile([P, D_IN], U8, name="w_scales%d" % n, align_bytes=64) for n in range(N_IN)]
         g_codes = [keep.tile([P, 512], U32, name="g_codes%d" % j, align_bytes=64) for j in range(8)]
@@ -152,7 +152,7 @@ def tile_transforming_t_kernel(tc, inputs, transform_mat, grad_out, out):
 
         def mm_pair(c):
             for tl in range(2):
-                res = stage.tile([P, 2048], F32, name="res")
+                res = stage.tile([P, 2048], F32, name="res", align_bytes=256)
                 for nl in range(2):
                     for half in range(2):
                         at = (nl * 2 + half) * 512
@@ -160,7 +160,7 @@ def tile_transforming_t_kernel(tc, inputs, transform_mat, grad_out, out):
                 nc.sync.dma_start(out=o_dram[2 * c + tl][:, 0:2048], in_=res[:])
 
         def mm_single(c, n):
-            res = stage.tile([P, 2048], F32, name="res")
+            res = stage.tile([P, 2048], F32, name="res", align_bytes=256)
             for tl in range(2):
                 for half in range(2):
                     at = (tl * 2 + half) * 512

@@ -24,6 +24,8 @@ BYTES = 2 * B * N_IN * K + 2 * N_IN * D_IN * K + 4 * B * N_IN * D_IN
 
 def tile_transforming_t_kernel(tc, inputs, transform_mat, grad_out, out):
     nc = tc.nc
+    w_late = transform_mat.rearrange("a (d e) m (h l) o x -> (a d) (m h) e (l o x)", d=2, h=4)[1]
+    g_late = grad_out.rearrange("(p d t) n m o x -> d p (t n m o x)", d=2, t=4)[1]
     w_dram = transform_mat.rearrange("a n m (h l) o x -> (a n) (m h) (l o x)", h=4)
     g_dram = grad_out.rearrange("(p c t) n m o x -> c p (t n m o x)", c=BC, t=2)
     o_dram = out.rearrange("(p t) n i x -> t p (n i x)", t=BT)
@@ -42,22 +44,24 @@ def tile_transforming_t_kernel(tc, inputs, transform_mat, grad_out, out):
         ident = keep.tile([P, P], F32, name="ident")
         make_identity(nc, ident[:])
 
-        w_raw = [keep.tile([P, 4096], BF16, name="w_raw%d" % n, align_bytes=256) for n in range(N_IN)]
-        g_raw = [keep.tile([P, 4096], BF16, name="g_raw%d" % c, align_bytes=256) for c in range(BC)]
+        w_first = [keep.tile([P, 4096], BF16, name="w_raw%d" % n, align_bytes=256) for n in range(2)]
+        g_first = [keep.tile([P, 4096], BF16, name="g_raw%d" % c, align_bytes=256) for c in range(2)]
+        w_second = keep.tile([P, 8192], BF16, name="w_second", align_bytes=256)
+        g_second = keep.tile([P, 8192], BF16, name="g_second", align_bytes=256)
+        w_raw = [w_first[0][:], w_first[1][:], w_second[:, 0:4096], w_second[:, 4096:8192]]
+        g_raw = [g_first[0][:], g_first[1][:], g_second[:, 0:4096], g_second[:, 4096:8192]]
         w_codes = [keep.tile([P, D_IN], U32, name="w_codes%d" % n, align_bytes=64) for n in range(N_IN)]
         w_scales = [keep.tile([P, D_IN], U8, name="w_scales%d" % n, align_bytes=64) for n in range(N_IN)]
         g_codes = [keep.tile([P, 512], U32, name="g_codes%d" % j, align_bytes=64) for j in range(8)]
         g_scales = [keep.tile([P, 512], U8, name="g_scales%d" % j, align_bytes=64) for j in range(8)]
 
         for h in range(2):
-            nc.sync.dma_start(out=w_raw[0][:, h * 2048 : h * 2048 + 2048], in_=w_dram[0][:, h * 2048 : h * 2048 + 2048])
-        nc.sync.dma_start(out=w_raw[1][:], in_=w_dram[1])
-        nc.sync.dma_start(out=g_raw[0][:], in_=g_dram[0])
-        nc.sync.dma_start(out=g_raw[1][:], in_=g_dram[1])
-        nc.sync.dma_start(out=g_raw[2][:], in_=g_dram[2])
-        nc.sync.dma_start(out=g_raw[3][:], in_=g_dram[3])
-        nc.sync.dma_start(out=w_raw[2][:], in_=w_dram[2])
-        nc.sync.dma_start(out=w_raw[3][:], in_=w_dram[3])
+            nc.sync.dma_start(out=w_first[0][:, h * 2048 : h * 2048 + 2048], in_=w_dram[0][:, h * 2048 : h * 2048 + 2048])
+        nc.sync.dma_start(out=w_first[1][:], in_=w_dram[1])
+        nc.sync.dma_start(out=g_first[0][:], in_=g_dram[0])
+        nc.sync.dma_start(out=g_first[1][:], in_=g_dram[1])
+        nc.sync.dma_start(out=g_second[:], in_=g_late)
+        nc.sync.dma_start(out=w_second[:].rearrange("p (e f) -> p e f", e=2), in_=w_late)
 
         def empty_bank(index, dst, src):
             if index % 2 == 0:
@@ -73,7 +77,7 @@ def tile_transforming_t_kernel(tc, inputs, transform_mat, grad_out, out):
         mid = {}
 
         def w_stage1(n):
-            words = w_raw[n][:].bitcast(F32).rearrange("p (h j o) -> p h j o", h=2, o=8)
+            words = w_raw[n].bitcast(F32).rearrange("p (h j o) -> p h j o", h=2, o=8)
             s2 = work.tile([P, 2048], F32, name="s2")
             mid[n] = s2
             s2v = s2[:].rearrange("p (a h m o) -> p a h m o", a=4, h=2, o=8)
@@ -106,7 +110,7 @@ def tile_transforming_t_kernel(tc, inputs, transform_mat, grad_out, out):
                 )
 
         def g_words(c):
-            return g_raw[c][:].bitcast(F32).rearrange("p (t n u q) -> p t n u q", t=2, n=N_IN, u=2)
+            return g_raw[c].bitcast(F32).rearrange("p (t n u q) -> p t n u q", t=2, n=N_IN, u=2)
 
         def g_quantize(slot, grouped):
             nc.vector.quantize_mx(

@@ -25,7 +25,6 @@ BYTES = 2 * B * N_IN * K + 2 * N_IN * D_IN * K + 4 * B * N_IN * D_IN
 def tile_transforming_t_kernel(tc, inputs, transform_mat, grad_out, out):
     nc = tc.nc
     w_late = transform_mat.rearrange("a (d e) m (h l) o x -> (a d) (m h) e (l o x)", d=2, h=4)[1]
-    g_late = grad_out.rearrange("(p d t) n m o x -> d p (t n m o x)", d=2, t=4)[1]
     w_dram = transform_mat.rearrange("a n m (h l) o x -> (a n) (m h) (l o x)", h=4)
     g_dram = grad_out.rearrange("(p c t) n m o x -> c p (t n m o x)", c=BC, t=2)
     o_dram = out.rearrange("(p t) n i x -> t p (n i x)", t=BT)
@@ -45,11 +44,10 @@ def tile_transforming_t_kernel(tc, inputs, transform_mat, grad_out, out):
         make_identity(nc, ident[:])
 
         w_first = [keep.tile([P, 4096], BF16, name="w_raw%d" % n, align_bytes=256) for n in range(2)]
-        g_first = [keep.tile([P, 4096], BF16, name="g_raw%d" % c, align_bytes=256) for c in range(2)]
+        g_first = [keep.tile([P, 4096], BF16, name="g_raw%d" % c, align_bytes=256) for c in range(BC)]
         w_second = keep.tile([P, 8192], BF16, name="w_second", align_bytes=256)
-        g_second = keep.tile([P, 8192], BF16, name="g_second", align_bytes=256)
         w_raw = [w_first[0][:], w_first[1][:], w_second[:, 0:4096], w_second[:, 4096:8192]]
-        g_raw = [g_first[0][:], g_first[1][:], g_second[:, 0:4096], g_second[:, 4096:8192]]
+        g_raw = [g_first[c][:] for c in range(BC)]
         w_codes = [keep.tile([P, D_IN], U32, name="w_codes%d" % n, align_bytes=64) for n in range(N_IN)]
         w_scales = [keep.tile([P, D_IN], U8, name="w_scales%d" % n, align_bytes=64) for n in range(N_IN)]
         g_codes = [keep.tile([P, 512], U32, name="g_codes%d" % j, align_bytes=64) for j in range(8)]
@@ -58,9 +56,8 @@ def tile_transforming_t_kernel(tc, inputs, transform_mat, grad_out, out):
         for h in range(2):
             nc.sync.dma_start(out=w_first[0][:, h * 2048 : h * 2048 + 2048], in_=w_dram[0][:, h * 2048 : h * 2048 + 2048])
         nc.sync.dma_start(out=w_first[1][:], in_=w_dram[1])
-        nc.sync.dma_start(out=g_first[0][:], in_=g_dram[0])
-        nc.sync.dma_start(out=g_first[1][:], in_=g_dram[1])
-        nc.sync.dma_start(out=g_second[:], in_=g_late)
+        for c in range(BC):
+            nc.sync.dma_start(out=g_first[c][:], in_=g_dram[c])
         nc.sync.dma_start(out=w_second[:].rearrange("p (e f) -> p e f", e=2), in_=w_late)
 
         def empty_bank(index, dst, src):

@@ -38,8 +38,6 @@ def tile_transforming_t_kernel(tc, inputs, transform_mat, grad_out, out):
         psum = ctx.enter_context(tc.psum_pool(name="psum", bufs=8))
         ctx.enter_context(tc.manual_schedule())
 
-        zeros = keep.tile([P, 512], BF16, name="zeros")
-        nc.vector.memset(zeros[:], 0.0)
         ident = keep.tile([P, P], F32, name="ident")
         make_identity(nc, ident[:])
 
@@ -65,11 +63,6 @@ def tile_transforming_t_kernel(tc, inputs, transform_mat, grad_out, out):
                 nc.scalar.copy(out=dst, in_=src)
             else:
                 nc.vector.tensor_copy(out=dst, in_=src)
-
-        def warm(count):
-            for unused in range(count):
-                ps = psum.tile([P, 512], F32, name="bank")
-                nc.tensor.matmul(ps[:], lhsT=zeros[:, 0:P], rhs=zeros[:], start=True, stop=True)
 
         mid = {}
 
@@ -171,9 +164,7 @@ def tile_transforming_t_kernel(tc, inputs, transform_mat, grad_out, out):
                 in_=res[:].rearrange("p (t i) -> p t i", t=2),
             )
 
-        warm(6)
         w_stage1(0)
-        warm(1)
         w_stage2(0)
         w_stage1(1)
         g_prep_pair(0)

from contextlib import ExitStack

import concourse.mybir as mybir
from concourse.masks import make_identity

F32 = mybir.dt.float32
BF16 = mybir.dt.bfloat16
U32 = mybir.dt.uint32
U8 = mybir.dt.uint8
E4X4 = mybir.dt.float8_e4m3fn_x4
E5X4 = mybir.dt.float8_e5m2_x4

P = 128
B = 1024
N_IN = 4
D_IN = 1024
K = 512
BT = B // P
BC = BT // 2

FLOPS = 2 * B * N_IN * D_IN * K
BYTES = 2 * B * N_IN * K + 2 * N_IN * D_IN * K + 4 * B * N_IN * D_IN


def tile_transforming_t_kernel(tc, inputs, transform_mat, grad_out, out):
    nc = tc.nc
    w_late = transform_mat.rearrange("a (d e) m (h l) o x -> (a d) (m h) e (l o x)", d=2, h=4)[1]
    w_dram = transform_mat.rearrange("a n m (h l) o x -> (a n) (m h) (l o x)", h=4)
    g_dram = grad_out.rearrange("(p c t) n m o x -> c p (t n m o x)", c=BC, t=2)
    o_dram = out.rearrange("(p t) n i x -> t p (n i x)", t=BT)
    o_couple = out.rearrange("(p c t) n i x -> c p t (n i x)", c=BC, t=2)

    with ExitStack() as ctx:
        keep = ctx.enter_context(tc.tile_pool(name="keep", bufs=1))
        work = ctx.enter_context(tc.tile_pool(name="work", bufs=2))
        gwork = ctx.enter_context(tc.tile_pool(name="gwork", bufs=3))
        stage = ctx.enter_context(tc.tile_pool(name="stage", bufs=8))
        psum = ctx.enter_context(tc.psum_pool(name="psum", bufs=8))
        ctx.enter_context(tc.manual_schedule())

        ident = keep.tile([P, P], F32, name="ident")
        make_identity(nc, ident[:])

        w_first = [keep.tile([P, 4096], BF16, name="w_raw%d" % n, align_bytes=256) for n in range(2)]
        g_first = [keep.tile([P, 4096], BF16, name="g_raw%d" % c, align_bytes=256) for c in range(BC)]
        w_second = keep.tile([P, 8192], BF16, name="w_second", align_bytes=256)
        w_raw = [w_first[0][:], w_first[1][:], w_second[:, 0:4096], w_second[:, 4096:8192]]
        g_raw = [g_first[c][:] for c in range(BC)]
        w_codes = [keep.tile([P, D_IN], U32, name="w_codes%d" % n, align_bytes=64) for n in range(N_IN)]
        w_scales = [keep.tile([P, D_IN], U8, name="w_scales%d" % n, align_bytes=64) for n in range(N_IN)]
        g_codes = [keep.tile([P, 512], U32, name="g_codes%d" % j, align_bytes=64) for j in range(8)]
        g_scales = [keep.tile([P, 512], U8, name="g_scales%d" % j, align_bytes=64) for j in range(8)]

        for h in range(2):
            nc.sync.dma_start(out=w_first[0][:, h * 2048 : h * 2048 + 2048], in_=w_dram[0][:, h * 2048 : h * 2048 + 2048])
        nc.sync.dma_start(out=w_first[1][:], in_=w_dram[1])
        for c in range(BC):
            nc.sync.dma_start(out=g_first[c][:], in_=g_dram[c])
        nc.sync.dma_start(out=w_second[:].rearrange("p (e f) -> p e f", e=2), in_=w_late)

        def empty_bank(index, dst, src):
            if index % 2 == 0:
                nc.scalar.copy(out=dst, in_=src)
            else:
                nc.vector.tensor_copy(out=dst, in_=src)

        mid = {}

        def w_stage1(n):
            words = w_raw[n].bitcast(F32).rearrange("p (h j o) -> p h j o", h=2, o=8)
            s2 = work.tile([P, 2048], F32, name="s2")
            mid[n] = s2
            s2v = s2[:].rearrange("p (a h m o) -> p a h m o", a=4, h=2, o=8)
            for h in range(2):
                for og in range(2):
                    bank = psum.tile([P, 4, P], F32, name="bank")
                    for oo in range(4):
                        nc.tensor.transpose(bank[:, oo, :], words[:, h, :, og * 4 + oo], ident[:])
                    empty_bank(
                        og,
                        s2v[:, :, h, :, og * 4 : og * 4 + 4],
                        bank[:].rearrange("p o (m a) -> p a m o", a=4),
                    )

        def w_stage2(n):
            s2v = mid[n][:].rearrange("p (a h u q) -> p a h u q", a=4, h=2, u=2)
            grouped = work.tile([P, 4096], BF16, name="w_grouped", align_bytes=64)
            gv = grouped[:].bitcast(F32).rearrange("p (a h j u) -> p a h j u", a=4, h=2, u=2)
            for a in range(4):
                bank = psum.tile([P, 2, 2, P], F32, name="bank")
                for h in range(2):
                    for u in range(2):
                        nc.tensor.transpose(bank[:, h, u, :], s2v[:, a, h, u, :], ident[:])
                empty_bank(a, gv[:, a], bank[:].rearrange("p h u j -> p h j u"))
            for half in range(2):
                nc.vector.quantize_mx(
                    out=w_codes[n][:, half * 512 : half * 512 + 512].bitcast(E4X4),
                    scales=w_scales[n][:, half * 512 : half * 512 + 512],
                    in_=grouped[:, half * 2048 : half * 2048 + 2048],
                )

        def g_words(c):
            return g_raw[c].bitcast(F32).rearrange("p (t n u q) -> p t n u q", t=2, n=N_IN, u=2)

        def g_quantize(slot, grouped):
            nc.vector.quantize_mx(
                out=g_codes[slot][:].bitcast(E5X4),
                scales=g_scales[slot][:],
                in_=grouped[:],
            )

        def g_prep_pair(c):
            grouped = gwork.tile([P, 2048], BF16, name="g_grouped", align_bytes=64)
            gv = grouped[:].bitcast(F32).rearrange("p (t n b u) -> p t n b u", t=2, n=2, u=2)
            for tl in range(2):
                bank = psum.tile([P, 2, 2, P], F32, name="bank")
                for nl in range(2):
                    for u in range(2):
                        nc.tensor.transpose(bank[:, nl, u, :], g_words(c)[:, tl, nl, u, :], ident[:])
                empty_bank(0, gv[:, tl], bank[:].rearrange("p n u b -> p n b u"))
            g_quantize(c, grouped)

        def g_prep_single(cc, n):
            grouped = gwork.tile([P, 2048], BF16, name="g_grouped", align_bytes=64)
            gv = grouped[:].bitcast(F32).rearrange("p (c t b u) -> p c t b u", c=2, t=2, u=2)
            for cl in range(2):
                bank = psum.tile([P, 2, 2, P], F32, name="bank")
                for tl in range(2):
                    for u in range(2):
                        nc.tensor.transpose(bank[:, tl, u, :], g_words(2 * cc + cl)[:, tl, n, u, :], ident[:])
                empty_bank(0, gv[:, cl], bank[:].rearrange("p t u b -> p t b u"))
            g_quantize(2 * n + cc, grouped)

        def product(slot, col, n, half, dst):
            ps = psum.tile([P, 512], F32, name="bank")
            nc.tensor.matmul_mx(
                out=ps[:],
                lhsT=g_codes[slot][:, col : col + P].bitcast(E5X4),
                lhsT_scale=g_scales[slot][:, col : col + P],
                rhs=w_codes[n][:, half * 512 : half * 512 + 512].bitcast(E4X4),
                rhs_scale=w_scales[n][:, half * 512 : half * 512 + 512],
                start=True,
                stop=True,
            )
            empty_bank(half, dst, ps[:])

        def mm_pair(c):
            for tl in range(2):
                res = stage.tile([P, 2048], F32, name="res", align_bytes=256)
                for nl in range(2):
                    for half in range(2):
                        at = (nl * 2 + half) * 512
                        product(c, (tl * 2 + nl) * P, nl, half, res[:, at : at + 512])
                nc.sync.dma_start(out=o_dram[2 * c + tl][:, 0:2048], in_=res[:])

        def mm_single(c, n):
            res = stage.tile([P, 2048], F32, name="res", align_bytes=256)
            for tl in range(2):
                for half in range(2):
                    at = (tl * 2 + half) * 512
                    product(2 * n + c // 2, ((c % 2) * 2 + tl) * P, n, half, res[:, at : at + 512])
            nc.sync.dma_start(
                out=o_couple[c][:, :, n * D_IN : n * D_IN + D_IN],
                in_=res[:].rearrange("p (t i) -> p t i", t=2),
            )

        w_stage1(0)
        w_stage2(0)
        w_stage1(1)
        g_prep_pair(0)
        w_stage2(1)
        g_prep_pair(1)
        mm_pair(0)
        g_prep_pair(2)
        mm_pair(1)
        g_prep_pair(3)
        w_stage1(2)
        mm_pair(2)
        w_stage2(2)
        g_prep_single(0, 2)
        mm_pair(3)
        mm_single(0, 2)
        g_prep_single(1, 2)
        w_stage1(3)
        mm_single(1, 2)
        mm_single(2, 2)
        w_stage2(3)
        g_prep_single(0, 3)
        mm_single(3, 2)
        mm_single(0, 3)
        g_prep_single(1, 3)
        mm_single(1, 3)
        mm_single(2, 3)
        mm_single(3, 3)
